import numpy as np
import ml_dtypes


def mxq(x, axis, fmt="e4m3"):
    dtype, down = {"e4m3": (ml_dtypes.float8_e4m3fn, 7), "e5m2": (ml_dtypes.float8_e5m2, 14)}[fmt]
    v = np.moveaxis(np.asarray(x, np.float32).astype(ml_dtypes.bfloat16).astype(np.float64), axis, -1)
    blocks = v.reshape(v.shape[:-1] + (-1, 32))
    amax = np.abs(blocks).max(-1, keepdims=True)
    byte = np.maximum(np.where(amax > 0, np.frexp(amax)[1] - 1 + 127, 0) - down, 1)
    scale = np.exp2(byte - 127.0)
    codes = (blocks / scale).astype(np.float32).astype(dtype).astype(np.float64)
    return np.moveaxis((codes * scale).reshape(v.shape), -1, axis)


WIDE = False


def mx_kscale(k):
    if not WIDE:
        return np.ones(k)
    levels = np.array([10, -10, 5, -5, 0])
    if k % 512:
        return np.exp2(np.random.permutation(np.resize(levels, k // 32))).repeat(32)
    a = np.empty((k // 512, 16))
    for p in range(k // 512):
        a[p, :8] = np.random.permutation(np.resize(levels, 8))
        for g in range(8):
            far = levels[np.abs(levels - a[p, g]) >= 10]
            a[p, g + 8] = far[np.random.randint(len(far))]
    return np.exp2(a.ravel()).repeat(32)


BF16 = ml_dtypes.bfloat16


def bf(x):
    return np.asarray(x, np.float32).astype(BF16)


def f64(x):
    return np.asarray(x).astype(np.float64)


B, SA, SB, D, H, DH = 1, 768, 256, 1024, 8, 128
S = SA + SB
EPS = 1e-6


def make_rope(s, dh):
    pos = np.arange(s, dtype=np.float64)
    inv_freq = 1.0 / (10000.0 ** (np.arange(0, dh, 2, dtype=np.float64) / dh))
    theta = pos[:, None] * inv_freq[None, :]
    cos, sin = np.cos(theta), np.sin(theta)
    row0 = np.stack([cos, -sin], axis=-1)
    row1 = np.stack([sin, cos], axis=-1)
    return np.stack([row0, row1], axis=-2)[None, None]


def rms_norm(x, w):
    return x * (1.0 / np.sqrt(np.mean(x * x, axis=-1, keepdims=True) + EPS)) * w


def apply_rope(x, freqs):
    x_ = x.reshape(*x.shape[:-1], -1, 1, 2)
    out = freqs[..., 0] * x_[..., 0] + freqs[..., 1] * x_[..., 1]
    return out.reshape(x.shape)


def qkv(x, w, b):
    y = (mxq(x, 2, "e4m3") @ mxq(w, 1, "e4m3").T) + b
    y = y.reshape(x.shape[0], x.shape[1], 3 * H, DH).transpose(0, 2, 1, 3)
    return y[:, :H], y[:, H:2 * H], y[:, 2 * H:]


def setup_inputs():
    sa, sb = mx_kscale(D), mx_kscale(D)
    return {
        "hidden_states_a": bf(np.random.standard_normal((B, SA, D)) * sa),
        "hidden_states_b": bf(np.random.standard_normal((B, SB, D)) * sb),
        "image_rotary_emb": bf(make_rope(S, DH)),
        "a_qkv_w": bf(np.random.standard_normal((3 * D, D)) / np.sqrt(D) / sa),
        "a_qkv_b": bf(np.random.standard_normal(3 * D) * 0.2),
        "b_qkv_w": bf(np.random.standard_normal((3 * D, D)) / np.sqrt(D) / sb),
        "b_qkv_b": bf(np.random.standard_normal(3 * D) * 0.2),
        "norm_q_a_w": bf(1.5 + 0.15 * np.random.standard_normal(DH)),
        "norm_k_a_w": bf(1.5 + 0.15 * np.random.standard_normal(DH)),
        "norm_q_b_w": bf(1.5 + 0.15 * np.random.standard_normal(DH)),
        "norm_k_b_w": bf(1.5 + 0.15 * np.random.standard_normal(DH)),
    }


def reference(hidden_states_a, hidden_states_b, image_rotary_emb, a_qkv_w, a_qkv_b, b_qkv_w, b_qkv_b,
              norm_q_a_w, norm_k_a_w, norm_q_b_w, norm_k_b_w):
    q_a, k_a, v_a = qkv(f64(hidden_states_a), f64(a_qkv_w), f64(a_qkv_b))
    q_a = rms_norm(q_a, f64(norm_q_a_w))
    k_a = rms_norm(k_a, f64(norm_k_a_w))
    q_b, k_b, v_b = qkv(f64(hidden_states_b), f64(b_qkv_w), f64(b_qkv_b))
    q_b = rms_norm(q_b, f64(norm_q_b_w))
    k_b = rms_norm(k_b, f64(norm_k_b_w))
    q = np.concatenate([q_b, q_a], axis=2)
    k = np.concatenate([k_b, k_a], axis=2)
    v = np.concatenate([v_b, v_a], axis=2)
    f = f64(image_rotary_emb)
    return apply_rope(q, f), apply_rope(k, f), v

@@ -1,0 +1,475 @@
+from contextlib import ExitStack
+
+import concourse.mybir as mybir
+from concourse.masks import make_identity
+
+FLOPS = 2 * 1024 * 1024 * 3072
+
+F32 = mybir.dt.float32
+BF16 = mybir.dt.bfloat16
+U32 = mybir.dt.uint32
+U8 = mybir.dt.uint8
+FP8X4 = mybir.dt.float8_e4m3fn_x4
+ACT = mybir.ActivationFunctionType
+ALU = mybir.AluOpType
+
+P = 128
+K = 1024
+HEADS = 16
+EPS = 1e-6
+TOKEN_BLOCKS = (6, 2)
+FIRST_BLOCK = (0, 6)
+BANK_PARTS = (((0, 512, 0, 0),), ((0, 256, 0, 1024), (256, 256, 1, 1536)))
+
+
+def x_word(blk, g):
+    if blk < 4:
+        return g * 512 + blk * P
+    if blk < 6:
+        return 1024 + g * 256 + (blk - 4) * P
+    return 1536 + g * 256 + (blk - 6) * P
+
+
+def tile_fluxjointattention_pa_kernel(
+    tc,
+    hidden_states_a,
+    hidden_states_b,
+    image_rotary_emb,
+    a_qkv_w,
+    a_qkv_b,
+    b_qkv_w,
+    b_qkv_b,
+    norm_q_a_w,
+    norm_k_a_w,
+    norm_q_b_w,
+    norm_k_b_w,
+    out_0,
+    out_1,
+    out_2,
+):
+    nc = tc.nc
+    with ExitStack() as ctx:
+        ctx.enter_context(tc.manual_schedule())
+        const = ctx.enter_context(tc.tile_pool(name="const", bufs=1))
+        raws = ctx.enter_context(tc.tile_pool(name="raws", bufs=4))
+        grps = ctx.enter_context(tc.tile_pool(name="grps", bufs=3))
+        cods = ctx.enter_context(tc.tile_pool(name="cods", bufs=4))
+        work = ctx.enter_context(tc.tile_pool(name="work", bufs=4))
+        outs = ctx.enter_context(tc.tile_pool(name="outs", bufs=2))
+        ps_prep = ctx.enter_context(tc.psum_pool(name="psprep", bufs=2))
+        ps_acc = ctx.enter_context(tc.psum_pool(name="psacc", bufs=2))
+        ps_y = ctx.enter_context(tc.psum_pool(name="psy", bufs=4))
+
+        xa_v = hidden_states_a.rearrange("o (p t) k -> p (o t) k", t=6)
+        xb_v = hidden_states_b.rearrange("o (p t) k -> p (o t) k", t=2)
+        w_v = [
+            a_qkv_w.rearrange("(n p) k -> p n k", p=P),
+            b_qkv_w.rearrange("(n p) k -> p n k", p=P),
+        ]
+        rope_v = image_rotary_emb.rearrange("a b s j i c -> (a b s) (j i c)")
+        biases = [a_qkv_b, b_qkv_b]
+        gains = [norm_q_a_w, norm_k_a_w, norm_q_b_w, norm_k_b_w]
+        qk_out = [out_0, out_1]
+
+        eps_t = const.tile([P, 1], F32, name="eps_t")
+        nc.vector.memset(eps_t[:], EPS)
+        warm = const.tile([P, 1], F32, name="warm")
+        nc.scalar.activation(out=warm[:], in_=eps_t[:], func=ACT.Abs_reciprocal_sqrt)
+        brow = const.tile([P, P], BF16, name="brow")
+        nc.vector.memset(brow[:], 0.0)
+        ident = const.tile([P, P], F32, name="ident")
+        make_identity(nc, ident[:])
+
+        vbias = const.tile([P, 2, 1024], BF16, name="vbias")
+        rope = const.tile([P, 8, 256], BF16, name="rope")
+        gain = const.tile([P, 4, P], BF16, name="gain")
+        for s in range(2):
+            nc.gpsimd.dma_start(
+                out=brow[16 * s : 16 * s + 16, :],
+                in_=biases[s][0:2048].rearrange("(r f) -> r f", f=P),
+            )
+        nc.gpsimd.dma_start(out=vbias[:, 0, :], in_=biases[0][2048:3072].partition_broadcast(P))
+        nc.gpsimd.dma_start(out=rope[:, 0:6, :], in_=rope_v[256:1024, :].rearrange("(p t) e -> p t e", t=6))
+        nc.gpsimd.dma_start(out=rope[:, 6:8, :], in_=rope_v[0:256, :].rearrange("(p t) e -> p t e", t=2))
+        for m in (0, 2, 1, 3):
+            nc.gpsimd.dma_start(out=gain[:, m, :], in_=gains[m].partition_broadcast(P))
+        nc.gpsimd.dma_start(out=vbias[:, 1, :], in_=biases[1][2048:3072].partition_broadcast(P))
+
+        def turn(pool, tag, rows):
+            bank = pool.tile([P, 512], F32, name="bank_" + tag, tag=tag)
+            words = rows.bitcast(F32)
+            for gu in range(4):
+                g, u = divmod(gu, 2)
+                nc.tensor.transpose(
+                    bank[:, gu * P : (gu + 1) * P], words[:, 256 * g + u : 256 * (g + 1) : 2], ident[:]
+                )
+            return bank
+
+        def leave(bank, dst):
+            nc.scalar.copy(out=dst, in_=bank[:].rearrange("p (g u n) -> p g n u", g=2, u=2))
+
+        def quant(codes, scales, grp, w0, w1, g0):
+            nc.vector.quantize_mx(
+                out=codes[:, w0:w1].bitcast(FP8X4),
+                scales=scales[:, w0:w1],
+                in_=grp[:, g0 : g0 + 4 * (w1 - w0)],
+            )
+
+        raw_w = {}
+
+        def load_w(s, chunk, j0, j1):
+            if j0 == 0:
+                if chunk < 4:
+                    raw_w[(s, chunk)] = raws.tile([P, 4, K], BF16, name="raw_w%d_%d" % (s, chunk), tag="raw")
+                else:
+                    raw_w[(s, chunk)] = raws.tile([P, 4, K], BF16, name="raw_w%d_%d" % (s, chunk), tag="rawv", bufs=2)
+            nc.sync.dma_start(out=raw_w[(s, chunk)][:, j0:j1, :], in_=w_v[s][:, 4 * chunk + j0 : 4 * chunk + j1, :])
+
+        raw_x = [raws.tile([P, 4, K], BF16, name="raw_x%d" % i, tag="raw") for i in range(2)]
+        x_codes = const.tile([P, 2048], U32, name="x_codes", align_bytes=64)
+        x_scale = const.tile([P, 2048], U8, name="x_scale", align_bytes=64)
+        xg = [grps.tile([P, 4096], BF16, name="xg%d" % i, tag="grp8", align_bytes=64) for i in range(2)]
+        xg0_v = xg[0][:].bitcast(F32).rearrange("p (g n u) -> p g n u", g=2, u=2)
+        xg1_v = xg[1][:].bitcast(F32).rearrange("p (c g n u) -> p c g n u", c=2, g=2, u=2)
+
+        def load_x(pair):
+            src = (xa_v[:, 0:2, :], xa_v[:, 2:4, :], xa_v[:, 4:6, :], xb_v)[pair]
+            nc.sync.dma_start(out=raw_x[pair // 2][:, 2 * (pair % 2) : 2 * (pair % 2) + 2, :], in_=src)
+
+        def x_prep(blk):
+            pool, tag = ((ps_prep, "prep"), (ps_y, "y"), (ps_y, "y"), (ps_prep, "prep"))[blk // 2]
+            bank = turn(pool, tag, raw_x[blk // 4][:, blk % 4, :])
+            if blk < 4:
+                leave(bank, xg0_v[:, :, blk * P : (blk + 1) * P, :])
+            else:
+                c, tb = divmod(blk - 4, 2)
+                leave(bank, xg1_v[:, c, :, tb * P : (tb + 1) * P, :])
+
+        def x_quant(c):
+            if c == 0:
+                quant(x_codes, x_scale, xg[0], 0, 1024, 0)
+            else:
+                quant(x_codes, x_scale, xg[1], 512 + 512 * c, 1024 + 512 * c, 2048 * (c - 1))
+
+        bias_t = const.tile([P, 32], F32, name="bias_t")
+
+        def bias_columns():
+            brow_f = const.tile([P, P], F32, name="brow_f")
+            nc.scalar.copy(out=brow_f[:], in_=brow[:])
+            bias_ps = ps_prep.tile([P, 512], F32, name="bias_ps", tag="prep")
+            nc.tensor.transpose(bias_ps[:, 0:P], brow_f[:], ident[:])
+            nc.scalar.copy(out=bias_t[:], in_=bias_ps[:, 0:32])
+
+        gain_p = gain[:].rearrange("p m (j c) -> p m j c", c=2)
+        tab = [const.tile([P, 8, 2, P], F32, name="tab%d" % kind) for kind in range(2)]
+        rope_q = rope[:].rearrange("p t (j q) -> p t j q", q=4)
+
+        def tables(kind):
+            for s in range(2):
+                b0 = FIRST_BLOCK[s]
+                b1 = b0 + TOKEN_BLOCKS[s]
+                g_bc = gain_p[:, 2 * s + kind, :, :].unsqueeze(1).to_broadcast([P, b1 - b0, 64, 2])
+                nc.vector.tensor_tensor(
+                    out=tab[kind][:, b0:b1, 0, :].rearrange("p t (j c) -> p t j c", c=2),
+                    in0=rope_q[:, b0:b1, :, 0:4:3],
+                    in1=g_bc,
+                    op=ALU.mult,
+                )
+                nc.vector.tensor_tensor(
+                    out=tab[kind][:, b0:b1, 1, :].rearrange("p t (j c) -> p t j c", c=2),
+                    in0=rope_q[:, b0:b1, :, 2:0:-1],
+                    in1=g_bc,
+                    op=ALU.mult,
+                )
+
+        vst = {}
+
+        def v_open(s, c):
+            vst[("grp", s, c)] = grps.tile([P, 4096], BF16, name="vg", tag="grp8", align_bytes=64)
+
+        def v_turn(s, c, j, pool, tag):
+            vst[("bank", s, c, j)] = turn(pool, tag, raw_w[(s, 4 + c)][:, j, :])
+
+        def v_leave(s, c, j):
+            vg_v = vst[("grp", s, c)][:].bitcast(F32).rearrange("p (g n u) -> p g n u", g=2, u=2)
+            leave(vst[("bank", s, c, j)], vg_v[:, :, j * P : (j + 1) * P, :])
+
+        def v_prep(s, c, j, pool, tag):
+            v_turn(s, c, j, pool, tag)
+            v_leave(s, c, j)
+
+        def v_quant(s, c):
+            vc = const.tile([P, 1024], U32, name="vc%d%d" % (s, c), align_bytes=64)
+            vs = const.tile([P, 1024], U8, name="vs%d%d" % (s, c), align_bytes=64)
+            quant(vc, vs, vst[("grp", s, c)], 0, 1024, 0)
+            vst[("codes", s, c)] = (vc, vs)
+            vst[("out", s, c)] = outs.tile([P, 4, TOKEN_BLOCKS[s], P], F32, name="ov%d" % s)
+
+        def v_mult(s, c, t, pool, tag):
+            vc, vs = vst[("codes", s, c)]
+            acc = pool.tile([P, 512], F32, name="vacc", tag=tag)
+            for g in range(2):
+                xo = x_word(FIRST_BLOCK[s] + t, g)
+                nc.tensor.matmul_mx(
+                    out=acc[:],
+                    lhsT=x_codes[:, xo : xo + P].bitcast(FP8X4),
+                    lhsT_scale=x_scale[:, xo : xo + P],
+                    rhs=vc[:, g * 512 : (g + 1) * 512].bitcast(FP8X4),
+                    rhs_scale=vs[:, g * 512 : (g + 1) * 512],
+                    start=(g == 0),
+                    stop=(g == 1),
+                )
+            vst[("acc", s, c, t)] = acc
+
+        def v_add(s, c, t):
+            nc.vector.tensor_tensor(
+                out=vst[("out", s, c)][:, :, t, :],
+                in0=vst[("acc", s, c, t)][:].rearrange("p (h f) -> p h f", h=4),
+                in1=vbias[:, s, c * 512 : (c + 1) * 512].rearrange("p (h f) -> p h f", h=4),
+                op=ALU.add,
+            )
+
+        def v_store(s, c):
+            lo, hi = ((256, 1024), (0, 256))[s]
+            nc.sync.dma_start(
+                out=out_2[0, 4 * c : 4 * c + 4, lo:hi, :].rearrange("h (p t) f -> p h (t f)", t=TOKEN_BLOCKS[s]),
+                in_=vst[("out", s, c)][:].rearrange("p h t f -> p h (t f)"),
+            )
+
+        def v_blocks(s, c, t0, t1):
+            for t in range(t0, t1):
+                v_mult(s, c, t, ps_acc, "acc")
+                v_add(s, c, t)
+
+        def v_blocks_ahead(s, c, t0, t1):
+            for t in range(t0, t1):
+                v_mult(s, c, t, ps_y, "y")
+            for t in range(t0, t1):
+                v_add(s, c, t)
+
+        st = {}
+
+        def qk_turn(h):
+            st[("grp", h)] = grps.tile([P, 2048], BF16, name="grp", tag="grp4", align_bytes=64, bufs=3)
+            for s in range(2):
+                st[("bank", h, s)] = turn(ps_prep, "prep", raw_w[(s, h // 4)][:, h % 4, :])
+
+        def qk_leave(h):
+            grp_v = st[("grp", h)][:].bitcast(F32).rearrange("p (s g n u) -> p s g n u", s=2, g=2, u=2)
+            for s in range(2):
+                leave(st[("bank", h, s)], grp_v[:, s, :, :, :])
+
+        def qk_quant(h):
+            wc = cods.tile([P, 512], U32, name="wc", align_bytes=64)
+            ws = cods.tile([P, 512], U8, name="ws", align_bytes=64)
+            quant(wc, ws, st[("grp", h)], 0, 512, 0)
+            st[("codes", h)] = (wc, ws)
+
+        def qk_mult(h, bank):
+            wc, ws = st[("codes", h)]
+            acc = ps_acc.tile([P, 512], F32, name="acc", tag="acc")
+            for c0, n, s, xw in BANK_PARTS[bank]:
+                for g in range(2):
+                    wo = (2 * s + g) * P
+                    xo = xw + g * n
+                    nc.tensor.matmul_mx(
+                        out=acc[:, c0 : c0 + n],
+                        lhsT=wc[:, wo : wo + P].bitcast(FP8X4),
+                        lhsT_scale=ws[:, wo : wo + P],
+                        rhs=x_codes[:, xo : xo + n].bitcast(FP8X4),
+                        rhs_scale=x_scale[:, xo : xo + n],
+                        start=(g == 0),
+                        stop=(g == 1),
+                    )
+            st[("acc", h, bank)] = acc
+
+        def qk_bias(h, bank):
+            acc = st[("acc", h, bank)]
+            yt = work.tile([P, 512], F32, name="yt")
+            for c0, n, s, xw in BANK_PARTS[bank]:
+                nc.scalar.activation(
+                    out=yt[:, c0 : c0 + n],
+                    in_=acc[:, c0 : c0 + n],
+                    func=ACT.Identity,
+                    bias=bias_t[:, 16 * s + h : 16 * s + h + 1],
+                    scale=1.0,
+                )
+            st[("yt", h, bank)] = yt
+
+        def qk_back(h, bank):
+            yt = st[("yt", h, bank)]
+            y = ps_y.tile([P, 512], F32, name="y", tag="y")
+            for b in range(2):
+                nc.tensor.matmul(
+                    out=y[:, b * P : (b + 1) * P], lhsT=yt[:, b * P : (b + 1) * P], rhs=ident[:], start=True, stop=True
+                )
+            for b in range(2, 4):
+                nc.tensor.transpose(y[:, b * P : (b + 1) * P], yt[:, b * P : (b + 1) * P], ident[:])
+            st[("y", h, bank)] = y
+
+        unused = const.tile([P, 8, P], BF16, name="unused")
+
+        def qk_square(h, bank):
+            if bank == 0:
+                st[("ss", h)] = work.tile([P, 8], F32, name="ss")
+            y = st[("y", h, bank)]
+            for b in range(4):
+                blk = 4 * bank + b
+                nc.scalar.activation(
+                    out=unused[:, blk, :],
+                    in_=y[:, b * P : (b + 1) * P],
+                    func=ACT.Square,
+                    accum_out=st[("ss", h)][:, blk : blk + 1],
+                )
+
+        def qk_rms(h):
+            rs = work.tile([P, 8], F32, name="rs")
+            nc.scalar.activation(
+                out=rs[:], in_=st[("ss", h)][:], func=ACT.Abs_reciprocal_sqrt, bias=eps_t[:], scale=1.0 / P
+            )
+            st[("rs", h)] = rs
+
+        def qk_rope(h, bank):
+            y = st[("y", h, bank)]
+            rs = st[("rs", h)]
+            mw = work.tile([P, 4, 2, P], F32, name="mw")
+            for b in range(4):
+                blk = 4 * bank + b
+                nc.vector.scalar_tensor_tensor(
+                    out=mw[:, b, :, :],
+                    in0=y[:, b * P : (b + 1) * P].unsqueeze(1).to_broadcast([P, 2, P]),
+                    scalar=rs[:, blk : blk + 1],
+                    in1=tab[h // 8][:, blk, :, :],
+                    op0=ALU.mult,
+                    op1=ALU.mult,
+                )
+            st[("m", h, bank)] = mw
+
+        def qk_add(h, bank):
+            if bank == 0:
+                st[("o", h)] = outs.tile([P, 8, P], F32, name="o", bufs=3)
+            mw = st[("m", h, bank)]
+            nc.vector.tensor_tensor(
+                out=st[("o", h)][:, 4 * bank : 4 * bank + 4, :].rearrange("p b (j c) -> p b j c", c=2),
+                in0=mw[:, :, 0, :].rearrange("p b (j c) -> p b j c", c=2),
+                in1=mw[:, :, 1, :].rearrange("p b (j c) -> p b j c", c=2)[:, :, :, ::-1],
+                op=ALU.add,
+            )
+
+        def qk_store(h):
+            dst = qk_out[h // 8]
+            o = st[("o", h)]
+            nc.sync.dma_start(
+                out=dst[0, h % 8, 256:1024, :].rearrange("(p t) f -> p (t f)", t=6),
+                in_=o[:, 0:6, :].rearrange("p t f -> p (t f)"),
+            )
+            nc.sync.dma_start(
+                out=dst[0, h % 8, 0:256, :].rearrange("(p t) f -> p (t f)", t=2),
+                in_=o[:, 6:8, :].rearrange("p t f -> p (t f)"),
+            )
+
+        load_x(0)
+        load_x(1)
+        load_w(0, 4, 0, 2)
+        load_w(0, 4, 2, 4)
+        load_x(2)
+        load_x(3)
+        load_w(0, 5, 0, 2)
+        load_w(0, 5, 2, 4)
+        for j in range(2):
+            for s in range(2):
+                load_w(s, 0, j, j + 1)
+        for s in range(2):
+            load_w(s, 0, 2, 4)
+
+        for blk in range(4):
+            x_prep(blk)
+        x_quant(0)
+        v_open(0, 0)
+        for j in range(4):
+            if j < 2:
+                v_prep(0, 0, j, ps_y, "y")
+            else:
+                v_prep(0, 0, j, ps_prep, "prep")
+        v_quant(0, 0)
+        for blk in range(4, 8):
+            x_prep(blk)
+        x_quant(1)
+        x_quant(2)
+        for s in range(2):
+            load_w(s, 1, 0, 4)
+        v_blocks(0, 0, 0, 2)
+        tables(0)
+        bias_columns()
+        v_open(0, 1)
+        for j in range(4):
+            v_prep(0, 1, j, ps_y, "y")
+        load_w(1, 4, 0, 4)
+        qk_turn(0)
+        qk_leave(0)
+        qk_quant(0)
+        v_blocks_ahead(0, 0, 2, 4)
+        tables(1)
+        qk_turn(1)
+        qk_leave(1)
+        qk_mult(0, 0)
+        qk_mult(0, 1)
+        qk_bias(0, 0)
+        qk_bias(0, 1)
+        qk_quant(1)
+        v_blocks_ahead(0, 0, 4, 6)
+        v_store(0, 0)
+        v_quant(0, 1)
+        load_w(1, 5, 0, 4)
+        qk_turn(2)
+        qk_leave(2)
+
+        for h in range(1, HEADS + 1):
+            qk_back(h - 1, 0)
+            qk_back(h - 1, 1)
+            if h < HEADS:
+                qk_mult(h, 0)
+                qk_mult(h, 1)
+            if h + 2 < HEADS:
+                qk_turn(h + 2)
+            elif h < HEADS:
+                if h + 2 == HEADS:
+                    v_open(1, 0)
+                for j in range(2):
+                    v_turn(1, 0, 2 * (h + 2 - HEADS) + j, ps_prep, "prep")
+            qk_square(h - 1, 0)
+            qk_square(h - 1, 1)
+            if h < HEADS:
+                qk_bias(h, 0)
+            qk_rms(h - 1)
+            if h < HEADS:
+                qk_bias(h, 1)
+            if h + 2 < HEADS:
+                qk_leave(h + 2)
+            elif h < HEADS:
+                for j in range(2):
+                    v_leave(1, 0, 2 * (h + 2 - HEADS) + j)
+            else:
+                v_open(1, 1)
+                for j in range(4):
+                    v_prep(1, 1, j, ps_prep, "prep")
+            if h + 1 < HEADS:
+                qk_quant(h + 1)
+            elif h == HEADS:
+                v_quant(1, 0)
+            qk_rope(h - 1, 0)
+            if h <= 3:
+                v_blocks(0, 1, 2 * h - 2, 2 * h)
+            if h == 3:
+                v_store(0, 1)
+            qk_rope(h - 1, 1)
+            qk_add(h - 1, 0)
+            qk_add(h - 1, 1)
+            qk_store(h - 1)
+            if h in (1, 5):
+                for s in range(2):
+                    load_w(s, (h + 7) // 4, 0, 4)
+        v_quant(1, 1)
+        for c in range(2):
+            v_blocks_ahead(1, c, 0, 2)
+            v_store(1, c)

@@ -349,7 +349,7 @@ def tile_fluxjointattention_pa_kernel(
             if bank == 0:
                 st[("o", h)] = outs.tile([P, 8, P], F32, name="o", bufs=3)
             mw = st[("m", h, bank)]
-            nc.vector.tensor_tensor(
+            nc.gpsimd.tensor_tensor(
                 out=st[("o", h)][:, 4 * bank : 4 * bank + 4, :].rearrange("p b (j c) -> p b j c", c=2),
                 in0=mw[:, :, 0, :].rearrange("p b (j c) -> p b j c", c=2),
                 in1=mw[:, :, 1, :].rearrange("p b (j c) -> p b j c", c=2)[:, :, :, ::-1],

@@ -19,15 +19,11 @@ HEADS = 16
 EPS = 1e-6
 TOKEN_BLOCKS = (6, 2)
 FIRST_BLOCK = (0, 6)
-BANK_PARTS = (((0, 512, 0, 0),), ((0, 256, 0, 1024), (256, 256, 1, 1536)))
+BIAS_PARTS = (((0, 512, 0),), ((0, 256, 0), (256, 256, 1)))
 
 
 def x_word(blk, g):
-    if blk < 4:
-        return g * 512 + blk * P
-    if blk < 6:
-        return 1024 + g * 256 + (blk - 4) * P
-    return 1536 + g * 256 + (blk - 6) * P
+    return (blk // 2) * 512 + g * 256 + (blk % 2) * P
 
 
 def tile_fluxjointattention_pa_kernel(
@@ -58,7 +54,8 @@ def tile_fluxjointattention_pa_kernel(
         outs = ctx.enter_context(tc.tile_pool(name="outs", bufs=2))
         ps_prep = ctx.enter_context(tc.psum_pool(name="psprep", bufs=2))
         ps_acc = ctx.enter_context(tc.psum_pool(name="psacc", bufs=2))
-        ps_y = ctx.enter_context(tc.psum_pool(name="psy", bufs=4))
+        ps_v = ctx.enter_context(tc.psum_pool(name="psv", bufs=1))
+        ps_y = ctx.enter_context(tc.psum_pool(name="psy", bufs=3))
 
         xa_v = hidden_states_a.rearrange("o (p t) k -> p (o t) k", t=6)
         xb_v = hidden_states_b.rearrange("o (p t) k -> p (o t) k", t=2)
@@ -71,29 +68,33 @@ def tile_fluxjointattention_pa_kernel(
         gains = [norm_q_a_w, norm_k_a_w, norm_q_b_w, norm_k_b_w]
         qk_out = [out_0, out_1]
 
+        gain = const.tile([P, 4, P], BF16, name="gain")
+        brow = const.tile([P, P], BF16, name="brow")
+        nc.vector.memset(brow[:], 0.0)
+        for s in range(2):
+            nc.scalar.dma_start(
+                out=brow[16 * s : 16 * s + 16, :],
+                in_=biases[s][0:2048].rearrange("(r f) -> r f", f=P),
+            )
+        for m in (0, 2):
+            nc.scalar.dma_start(out=gain[:, m, :], in_=gains[m].partition_broadcast(P))
         eps_t = const.tile([P, 1], F32, name="eps_t")
         nc.vector.memset(eps_t[:], EPS)
         warm = const.tile([P, 1], F32, name="warm")
         nc.scalar.activation(out=warm[:], in_=eps_t[:], func=ACT.Abs_reciprocal_sqrt)
-        brow = const.tile([P, P], BF16, name="brow")
-        nc.vector.memset(brow[:], 0.0)
         ident = const.tile([P, P], F32, name="ident")
         make_identity(nc, ident[:])
 
         vbias = const.tile([P, 2, 1024], BF16, name="vbias")
         rope = const.tile([P, 8, 256], BF16, name="rope")
-        gain = const.tile([P, 4, P], BF16, name="gain")
         for s in range(2):
-            nc.gpsimd.dma_start(
-                out=brow[16 * s : 16 * s + 16, :],
-                in_=biases[s][0:2048].rearrange("(r f) -> r f", f=P),
-            )
-        nc.gpsimd.dma_start(out=vbias[:, 0, :], in_=biases[0][2048:3072].partition_broadcast(P))
-        nc.gpsimd.dma_start(out=rope[:, 0:6, :], in_=rope_v[256:1024, :].rearrange("(p t) e -> p t e", t=6))
-        nc.gpsimd.dma_start(out=rope[:, 6:8, :], in_=rope_v[0:256, :].rearrange("(p t) e -> p t e", t=2))
-        for m in (0, 2, 1, 3):
+            nc.gpsimd.dma_start(out=vbias[:, s, :], in_=biases[s][2048:3072].partition_broadcast(P))
+        for m in (1, 3):
             nc.gpsimd.dma_start(out=gain[:, m, :], in_=gains[m].partition_broadcast(P))
-        nc.gpsimd.dma_start(out=vbias[:, 1, :], in_=biases[1][2048:3072].partition_broadcast(P))
+
+        def load_rope():
+            nc.sync.dma_start(out=rope[:, 0:6, :], in_=rope_v[256:1024, :].rearrange("(p t) e -> p t e", t=6))
+            nc.sync.dma_start(out=rope[:, 6:8, :], in_=rope_v[0:256, :].rearrange("(p t) e -> p t e", t=2))
 
         def turn(pool, tag, rows):
             bank = pool.tile([P, 512], F32, name="bank_" + tag, tag=tag)
@@ -105,8 +106,12 @@ def tile_fluxjointattention_pa_kernel(
                 )
             return bank
 
-        def leave(bank, dst):
-            nc.scalar.copy(out=dst, in_=bank[:].rearrange("p (g u n) -> p g n u", g=2, u=2))
+        def leave(bank, dst, vector=False):
+            words = bank[:].rearrange("p (g u n) -> p g n u", g=2, u=2)
+            if vector:
+                nc.vector.tensor_copy(out=dst, in_=words)
+            else:
+                nc.scalar.copy(out=dst, in_=words)
 
         def quant(codes, scales, grp, w0, w1, g0):
             nc.vector.quantize_mx(
@@ -129,34 +134,26 @@ def tile_fluxjointattention_pa_kernel(
         x_codes = const.tile([P, 2048], U32, name="x_codes", align_bytes=64)
         x_scale = const.tile([P, 2048], U8, name="x_scale", align_bytes=64)
         xg = [grps.tile([P, 4096], BF16, name="xg%d" % i, tag="grp8", align_bytes=64) for i in range(2)]
-        xg0_v = xg[0][:].bitcast(F32).rearrange("p (g n u) -> p g n u", g=2, u=2)
-        xg1_v = xg[1][:].bitcast(F32).rearrange("p (c g n u) -> p c g n u", c=2, g=2, u=2)
 
         def load_x(pair):
             src = (xa_v[:, 0:2, :], xa_v[:, 2:4, :], xa_v[:, 4:6, :], xb_v)[pair]
             nc.sync.dma_start(out=raw_x[pair // 2][:, 2 * (pair % 2) : 2 * (pair % 2) + 2, :], in_=src)
 
-        def x_prep(blk):
-            pool, tag = ((ps_prep, "prep"), (ps_y, "y"), (ps_y, "y"), (ps_prep, "prep"))[blk // 2]
+        def x_prep(blk, vector):
+            pool, tag = ((ps_y, "y"), (ps_prep, "prep"), (ps_acc, "acc"), (ps_y, "y"))[blk // 2]
             bank = turn(pool, tag, raw_x[blk // 4][:, blk % 4, :])
-            if blk < 4:
-                leave(bank, xg0_v[:, :, blk * P : (blk + 1) * P, :])
-            else:
-                c, tb = divmod(blk - 4, 2)
-                leave(bank, xg1_v[:, c, :, tb * P : (tb + 1) * P, :])
+            pairs = xg[blk // 4][:].bitcast(F32).rearrange("p (c g n u) -> p c g n u", c=2, g=2, u=2)
+            leave(bank, pairs[:, (blk // 2) % 2, :, (blk % 2) * P : (blk % 2 + 1) * P, :], vector)
 
-        def x_quant(c):
-            if c == 0:
-                quant(x_codes, x_scale, xg[0], 0, 1024, 0)
-            else:
-                quant(x_codes, x_scale, xg[1], 512 + 512 * c, 1024 + 512 * c, 2048 * (c - 1))
+        def x_quant(pair):
+            quant(x_codes, x_scale, xg[pair // 2], 512 * pair, 512 * pair + 512, 2048 * (pair % 2))
 
         bias_t = const.tile([P, 32], F32, name="bias_t")
 
         def bias_columns():
             brow_f = const.tile([P, P], F32, name="brow_f")
             nc.scalar.copy(out=brow_f[:], in_=brow[:])
-            bias_ps = ps_prep.tile([P, 512], F32, name="bias_ps", tag="prep")
+            bias_ps = ps_v.tile([P, 512], F32, name="bias_ps", tag="vacc")
             nc.tensor.transpose(bias_ps[:, 0:P], brow_f[:], ident[:])
             nc.scalar.copy(out=bias_t[:], in_=bias_ps[:, 0:32])
 
@@ -164,23 +161,15 @@ def tile_fluxjointattention_pa_kernel(
         tab = [const.tile([P, 8, 2, P], F32, name="tab%d" % kind) for kind in range(2)]
         rope_q = rope[:].rearrange("p t (j q) -> p t j q", q=4)
 
-        def tables(kind):
-            for s in range(2):
-                b0 = FIRST_BLOCK[s]
-                b1 = b0 + TOKEN_BLOCKS[s]
-                g_bc = gain_p[:, 2 * s + kind, :, :].unsqueeze(1).to_broadcast([P, b1 - b0, 64, 2])
-                nc.vector.tensor_tensor(
-                    out=tab[kind][:, b0:b1, 0, :].rearrange("p t (j c) -> p t j c", c=2),
-                    in0=rope_q[:, b0:b1, :, 0:4:3],
-                    in1=g_bc,
-                    op=ALU.mult,
-                )
-                nc.vector.tensor_tensor(
-                    out=tab[kind][:, b0:b1, 1, :].rearrange("p t (j c) -> p t j c", c=2),
-                    in0=rope_q[:, b0:b1, :, 2:0:-1],
-                    in1=g_bc,
-                    op=ALU.mult,
-                )
+        def table(engine, kind, s, c):
+            b0 = FIRST_BLOCK[s]
+            b1 = b0 + TOKEN_BLOCKS[s]
+            engine.tensor_tensor(
+                out=tab[kind][:, b0:b1, c, :].rearrange("p t (j c) -> p t j c", c=2),
+                in0=rope_q[:, b0:b1, :, (slice(0, 4, 3), slice(2, 0, -1))[c]],
+                in1=gain_p[:, 2 * s + kind, :, :].unsqueeze(1).to_broadcast([P, b1 - b0, 64, 2]),
+                op=ALU.mult,
+            )
 
         vst = {}
 
@@ -193,10 +182,6 @@ def tile_fluxjointattention_pa_kernel(
         def v_leave(s, c, j):
             vg_v = vst[("grp", s, c)][:].bitcast(F32).rearrange("p (g n u) -> p g n u", g=2, u=2)
             leave(vst[("bank", s, c, j)], vg_v[:, :, j * P : (j + 1) * P, :])
-
-        def v_prep(s, c, j, pool, tag):
-            v_turn(s, c, j, pool, tag)
-            v_leave(s, c, j)
 
         def v_quant(s, c):
             vc = const.tile([P, 1024], U32, name="vc%d%d" % (s, c), align_bytes=64)
@@ -236,48 +221,38 @@ def tile_fluxjointattention_pa_kernel(
                 in_=vst[("out", s, c)][:].rearrange("p h t f -> p h (t f)"),
             )
 
-        def v_blocks(s, c, t0, t1):
-            for t in range(t0, t1):
-                v_mult(s, c, t, ps_acc, "acc")
-                v_add(s, c, t)
-
-        def v_blocks_ahead(s, c, t0, t1):
-            for t in range(t0, t1):
-                v_mult(s, c, t, ps_y, "y")
-            for t in range(t0, t1):
-                v_add(s, c, t)
-
         st = {}
 
-        def qk_turn(h):
-            st[("grp", h)] = grps.tile([P, 2048], BF16, name="grp", tag="grp4", align_bytes=64, bufs=3)
-            for s in range(2):
-                st[("bank", h, s)] = turn(ps_prep, "prep", raw_w[(s, h // 4)][:, h % 4, :])
+        def qk_turn(h, s):
+            st[("bank", h, s)] = turn(ps_prep, "prep", raw_w[(s, h // 4)][:, h % 4, :])
 
-        def qk_leave(h):
+        def qk_leave(h, s, vector=False):
+            if s == 0:
+                st[("grp", h)] = grps.tile([P, 2048], BF16, name="grp", tag="grp4", align_bytes=64, bufs=3)
             grp_v = st[("grp", h)][:].bitcast(F32).rearrange("p (s g n u) -> p s g n u", s=2, g=2, u=2)
-            for s in range(2):
-                leave(st[("bank", h, s)], grp_v[:, s, :, :, :])
+            leave(st[("bank", h, s)], grp_v[:, s, :, :, :], vector)
 
-        def qk_quant(h):
-            wc = cods.tile([P, 512], U32, name="wc", align_bytes=64)
-            ws = cods.tile([P, 512], U8, name="ws", align_bytes=64)
-            quant(wc, ws, st[("grp", h)], 0, 512, 0)
-            st[("codes", h)] = (wc, ws)
+        def qk_quant(h, s0=0, s1=2):
+            if s0 == 0:
+                wc = cods.tile([P, 512], U32, name="wc", align_bytes=64)
+                ws = cods.tile([P, 512], U8, name="ws", align_bytes=64)
+                st[("codes", h)] = (wc, ws)
+            quant(*st[("codes", h)], st[("grp", h)], 256 * s0, 256 * s1, 1024 * s0)
 
         def qk_mult(h, bank):
             wc, ws = st[("codes", h)]
             acc = ps_acc.tile([P, 512], F32, name="acc", tag="acc")
-            for c0, n, s, xw in BANK_PARTS[bank]:
+            for half in range(2):
+                s = int(2 * bank + half == 3)
                 for g in range(2):
                     wo = (2 * s + g) * P
-                    xo = xw + g * n
+                    xo = x_word(4 * bank + 2 * half, g)
                     nc.tensor.matmul_mx(
-                        out=acc[:, c0 : c0 + n],
+                        out=acc[:, half * 256 : (half + 1) * 256],
                         lhsT=wc[:, wo : wo + P].bitcast(FP8X4),
                         lhsT_scale=ws[:, wo : wo + P],
-                        rhs=x_codes[:, xo : xo + n].bitcast(FP8X4),
-                        rhs_scale=x_scale[:, xo : xo + n],
+                        rhs=x_codes[:, xo : xo + 256].bitcast(FP8X4),
+                        rhs_scale=x_scale[:, xo : xo + 256],
                         start=(g == 0),
                         stop=(g == 1),
                     )
@@ -286,7 +261,7 @@ def tile_fluxjointattention_pa_kernel(
         def qk_bias(h, bank):
             acc = st[("acc", h, bank)]
             yt = work.tile([P, 512], F32, name="yt")
-            for c0, n, s, xw in BANK_PARTS[bank]:
+            for c0, n, s in BIAS_PARTS[bank]:
                 nc.scalar.activation(
                     out=yt[:, c0 : c0 + n],
                     in_=acc[:, c0 : c0 + n],
@@ -299,11 +274,11 @@ def tile_fluxjointattention_pa_kernel(
         def qk_back(h, bank):
             yt = st[("yt", h, bank)]
             y = ps_y.tile([P, 512], F32, name="y", tag="y")
-            for b in range(2):
+            for b in range(1):
                 nc.tensor.matmul(
                     out=y[:, b * P : (b + 1) * P], lhsT=yt[:, b * P : (b + 1) * P], rhs=ident[:], start=True, stop=True
                 )
-            for b in range(2, 4):
+            for b in range(1, 4):
                 nc.tensor.transpose(y[:, b * P : (b + 1) * P], yt[:, b * P : (b + 1) * P], ident[:])
             st[("y", h, bank)] = y
 
@@ -322,12 +297,16 @@ def tile_fluxjointattention_pa_kernel(
                     accum_out=st[("ss", h)][:, blk : blk + 1],
                 )
 
-        def qk_rms(h):
-            rs = work.tile([P, 8], F32, name="rs")
+        def qk_rms(h, bank):
+            if bank == 0:
+                st[("rs", h)] = work.tile([P, 8], F32, name="rs")
             nc.scalar.activation(
-                out=rs[:], in_=st[("ss", h)][:], func=ACT.Abs_reciprocal_sqrt, bias=eps_t[:], scale=1.0 / P
+                out=st[("rs", h)][:, 4 * bank : 4 * bank + 4],
+                in_=st[("ss", h)][:, 4 * bank : 4 * bank + 4],
+                func=ACT.Abs_reciprocal_sqrt,
+                bias=eps_t[:],
+                scale=1.0 / P,
             )
-            st[("rs", h)] = rs
 
         def qk_rope(h, bank):
             y = st[("y", h, bank)]
@@ -349,7 +328,8 @@ def tile_fluxjointattention_pa_kernel(
             if bank == 0:
                 st[("o", h)] = outs.tile([P, 8, P], F32, name="o", bufs=3)
             mw = st[("m", h, bank)]
-            nc.gpsimd.tensor_tensor(
+            engine = nc.vector if (h, bank) == (HEADS - 1, 1) else nc.gpsimd
+            engine.tensor_tensor(
                 out=st[("o", h)][:, 4 * bank : 4 * bank + 4, :].rearrange("p b (j c) -> p b j c", c=2),
                 in0=mw[:, :, 0, :].rearrange("p b (j c) -> p b j c", c=2),
                 in1=mw[:, :, 1, :].rearrange("p b (j c) -> p b j c", c=2)[:, :, :, ::-1],
@@ -370,106 +350,109 @@ def tile_fluxjointattention_pa_kernel(
 
         load_x(0)
         load_x(1)
-        load_w(0, 4, 0, 2)
-        load_w(0, 4, 2, 4)
+        for s in range(2):
+            load_w(s, 0, 0, 1)
         load_x(2)
         load_x(3)
-        load_w(0, 5, 0, 2)
-        load_w(0, 5, 2, 4)
-        for j in range(2):
-            for s in range(2):
-                load_w(s, 0, j, j + 1)
+        for s in range(2):
+            load_w(s, 0, 1, 2)
+        load_rope()
         for s in range(2):
             load_w(s, 0, 2, 4)
+        load_w(0, 4, 0, 4)
 
-        for blk in range(4):
-            x_prep(blk)
-        x_quant(0)
-        v_open(0, 0)
-        for j in range(4):
-            if j < 2:
-                v_prep(0, 0, j, ps_y, "y")
-            else:
-                v_prep(0, 0, j, ps_prep, "prep")
-        v_quant(0, 0)
-        for blk in range(4, 8):
-            x_prep(blk)
-        x_quant(1)
-        x_quant(2)
+        def x_pair(pair):
+            for blk in (2 * pair, 2 * pair + 1):
+                x_prep(blk, blk % 2 == 1 and pair < 3)
+            x_quant(pair)
+
+        x_pair(0)
+        x_pair(1)
+        for s in range(2):
+            qk_turn(0, s)
+            qk_leave(0, s, s == 1)
+        qk_quant(0)
+        bias_columns()
+        x_pair(2)
+        x_pair(3)
         for s in range(2):
             load_w(s, 1, 0, 4)
-        v_blocks(0, 0, 0, 2)
-        tables(0)
-        bias_columns()
-        v_open(0, 1)
-        for j in range(4):
-            v_prep(0, 1, j, ps_y, "y")
-        load_w(1, 4, 0, 4)
-        qk_turn(0)
-        qk_leave(0)
-        qk_quant(0)
-        v_blocks_ahead(0, 0, 2, 4)
-        tables(1)
-        qk_turn(1)
-        qk_leave(1)
-        qk_mult(0, 0)
-        qk_mult(0, 1)
-        qk_bias(0, 0)
-        qk_bias(0, 1)
-        qk_quant(1)
-        v_blocks_ahead(0, 0, 4, 6)
-        v_store(0, 0)
-        v_quant(0, 1)
-        load_w(1, 5, 0, 4)
-        qk_turn(2)
-        qk_leave(2)
+        load_w(0, 5, 0, 4)
 
-        for h in range(1, HEADS + 1):
-            qk_back(h - 1, 0)
-            qk_back(h - 1, 1)
-            if h < HEADS:
-                qk_mult(h, 0)
-                qk_mult(h, 1)
-            if h + 2 < HEADS:
-                qk_turn(h + 2)
-            elif h < HEADS:
-                if h + 2 == HEADS:
-                    v_open(1, 0)
-                for j in range(2):
-                    v_turn(1, 0, 2 * (h + 2 - HEADS) + j, ps_prep, "prep")
-            qk_square(h - 1, 0)
-            qk_square(h - 1, 1)
-            if h < HEADS:
-                qk_bias(h, 0)
-            qk_rms(h - 1)
-            if h < HEADS:
-                qk_bias(h, 1)
-            if h + 2 < HEADS:
-                qk_leave(h + 2)
-            elif h < HEADS:
-                for j in range(2):
-                    v_leave(1, 0, 2 * (h + 2 - HEADS) + j)
-            else:
-                v_open(1, 1)
-                for j in range(4):
-                    v_prep(1, 1, j, ps_prep, "prep")
-            if h + 1 < HEADS:
-                qk_quant(h + 1)
-            elif h == HEADS:
-                v_quant(1, 0)
-            qk_rope(h - 1, 0)
-            if h <= 3:
-                v_blocks(0, 1, 2 * h - 2, 2 * h)
-            if h == 3:
-                v_store(0, 1)
-            qk_rope(h - 1, 1)
-            qk_add(h - 1, 0)
-            qk_add(h - 1, 1)
-            qk_store(h - 1)
-            if h in (1, 5):
+        units = [(0, 0), (0, 1), (1, 0), (1, 1)]
+        prep_steps = list(range(2, 28, 2)) + [27, 28, 29]
+        quant_steps = [10, 18, 26, 31]
+        block_steps = list(range(11, 31, 2)) + [28, 30, 31, 32, 32, 33]
+        v_rows = [(s, c, j) for s, c in units for j in range(4)]
+        v_prods = [(s, c, t) for s, c in units for t in range(TOKEN_BLOCKS[s])]
+
+        steps = 2 * HEADS
+        for k in range(steps + 2):
+            rows = [v_rows[i] for i in range(16) if prep_steps[i] == k]
+            rows_before = [v_rows[i] for i in range(16) if prep_steps[i] == k - 1]
+            prods = [v_prods[i] for i in range(16) if block_steps[i] == k]
+            prods_before = [v_prods[i] for i in range(16) if block_steps[i] == k - 1]
+            ahead = divmod(k + 4, 2)
+            ahead_before = divmod(k + 3, 2)
+            if k % 2 == 1 and k + 1 < steps:
+                qk_quant((k + 1) // 2)
+            for prod in prods_before:
+                v_add(*prod)
+                if prod[2] == TOKEN_BLOCKS[prod[0]] - 1:
+                    v_store(prod[0], prod[1])
+            if k in quant_steps:
+                v_quant(*units[quant_steps.index(k)])
+            if k < 2:
+                for c in range(2):
+                    table(nc.vector, 0, k, c)
+            if k < steps:
+                qk_mult(k // 2, k % 2)
+            if k == 0:
+                qk_turn(1, 0)
+                qk_turn(1, 1)
+            if k < steps:
+                for i, prod in enumerate(prods):
+                    v_mult(*prod, *((ps_v, "vacc") if i == 0 else (ps_acc, "acc")))
+            if 0 < k <= steps:
+                qk_back((k - 1) // 2, (k - 1) % 2)
+            if k >= steps:
+                for i, prod in enumerate(prods):
+                    v_mult(*prod, *((ps_v, "vacc") if i == 0 else (ps_acc, "acc")))
+            if 0 < k and ahead[0] < HEADS:
+                if k == 1:
+                    qk_turn(2, 0)
+                qk_turn(*ahead)
+            if k == 0:
+                qk_leave(1, 0)
+            if k >= 2:
+                qk_square((k - 2) // 2, k % 2)
+            if k != 1 and ahead_before[0] < HEADS:
+                if k == 2:
+                    qk_leave(2, 0)
+                qk_leave(*ahead_before)
+            if k >= 2:
+                qk_rms((k - 2) // 2, k % 2)
+            if k < steps:
+                qk_bias(k // 2, k % 2)
+            for s, c, j in rows:
+                if j == 0:
+                    v_open(s, c)
+                v_turn(s, c, j, ps_prep, "prep")
+            for s, c, j in rows_before:
+                v_leave(s, c, j)
+            if k >= 2:
+                qk_rope((k - 2) // 2, k % 2)
+                if k in (4, 6, 8, 10):
+                    table(nc.gpsimd, 1, (k - 4) // 4, (k // 2) % 2)
+                qk_add((k - 2) // 2, k % 2)
+                if k % 2 == 1:
+                    qk_store((k - 2) // 2)
+            if k in (4, 12):
                 for s in range(2):
-                    load_w(s, (h + 7) // 4, 0, 4)
-        v_quant(1, 1)
-        for c in range(2):
-            v_blocks_ahead(1, c, 0, 2)
-            v_store(1, c)
+                    load_w(s, 2 + k // 12, 0, 4)
+            if k in (7, 15):
+                load_w(1, 4 + k // 15, 0, 4)
+        for i in range(16):
+            if block_steps[i] == steps + 1:
+                v_add(*v_prods[i])
+        v_store(1, 1)

@@ -68,29 +68,54 @@ def tile_fluxjointattention_pa_kernel(
         gains = [norm_q_a_w, norm_k_a_w, norm_q_b_w, norm_k_b_w]
         qk_out = [out_0, out_1]
 
-        gain = const.tile([P, 4, P], BF16, name="gain")
+        eps_t = const.tile([P, 1], F32, name="eps_t")
+        nc.vector.memset(eps_t[:], EPS)
+        warm = const.tile([P, 1], F32, name="warm")
+        nc.scalar.activation(out=warm[:], in_=eps_t[:], func=ACT.Abs_reciprocal_sqrt)
         brow = const.tile([P, P], BF16, name="brow")
         nc.vector.memset(brow[:], 0.0)
+        small = const.tile([P, 512], BF16, name="small")
+        nc.vector.memset(small[:], 0.0)
         for s in range(2):
             nc.scalar.dma_start(
                 out=brow[16 * s : 16 * s + 16, :],
                 in_=biases[s][0:2048].rearrange("(r f) -> r f", f=P),
             )
-        for m in (0, 2):
-            nc.scalar.dma_start(out=gain[:, m, :], in_=gains[m].partition_broadcast(P))
-        eps_t = const.tile([P, 1], F32, name="eps_t")
-        nc.vector.memset(eps_t[:], EPS)
-        warm = const.tile([P, 1], F32, name="warm")
-        nc.scalar.activation(out=warm[:], in_=eps_t[:], func=ACT.Abs_reciprocal_sqrt)
+        for m in range(4):
+            nc.scalar.dma_start(out=small[0:1, m * P : (m + 1) * P], in_=gains[m].unsqueeze(0))
+        for s in range(2):
+            nc.scalar.dma_start(
+                out=small[1 + 2 * s : 3 + 2 * s, :], in_=biases[s][2048:3072].rearrange("(r f) -> r f", f=512)
+            )
         ident = const.tile([P, P], F32, name="ident")
         make_identity(nc, ident[:])
+        ident_b = const.tile([P, P], BF16, name="ident_b")
+        nc.vector.tensor_copy(out=ident_b[:], in_=ident[:])
 
+        gain = const.tile([P, 4, P], BF16, name="gain")
         vbias = const.tile([P, 2, 1024], BF16, name="vbias")
         rope = const.tile([P, 8, 256], BF16, name="rope")
-        for s in range(2):
-            nc.gpsimd.dma_start(out=vbias[:, s, :], in_=biases[s][2048:3072].partition_broadcast(P))
-        for m in (1, 3):
-            nc.gpsimd.dma_start(out=gain[:, m, :], in_=gains[m].partition_broadcast(P))
+
+        def spread(bank, row):
+            nc.tensor.matmul(
+                out=bank, lhsT=ident_b[:, row : row + 1].to_broadcast([P, P]), rhs=small[:], start=True, stop=True
+            )
+
+        def spread_gains():
+            bank = ps_v.tile([P, 512], BF16, name="bank_gain", tag="vacc")
+            spread(bank[:], 0)
+            nc.vector.tensor_copy(out=gain[:].rearrange("p m f -> p (m f)"), in_=bank[:])
+
+        def spread_vbias(s):
+            bank = ps_v.tile([P, 1024], BF16, name="bank_vbias", tag="vacc")
+            for c in range(2):
+                spread(bank[:, c * 512 : (c + 1) * 512], 1 + 2 * s + c)
+            st[("vbias", s)] = bank
+
+        def vbias_leave(s):
+            nc.scalar.copy(out=vbias[:, s, :], in_=st[("vbias", s)][:])
+
+        st = {}
 
         def load_rope():
             nc.sync.dma_start(out=rope[:, 0:6, :], in_=rope_v[256:1024, :].rearrange("(p t) e -> p t e", t=6))
@@ -220,8 +245,6 @@ def tile_fluxjointattention_pa_kernel(
                 out=out_2[0, 4 * c : 4 * c + 4, lo:hi, :].rearrange("h (p t) f -> p h (t f)", t=TOKEN_BLOCKS[s]),
                 in_=vst[("out", s, c)][:].rearrange("p h t f -> p h (t f)"),
             )
-
-        st = {}
 
         def qk_turn(h, s):
             st[("bank", h, s)] = turn(ps_prep, "prep", raw_w[(s, h // 4)][:, h % 4, :])
@@ -375,6 +398,7 @@ def tile_fluxjointattention_pa_kernel(
         bias_columns()
         x_pair(2)
         x_pair(3)
+        spread_gains()
         for s in range(2):
             load_w(s, 1, 0, 4)
         load_w(0, 5, 0, 4)
@@ -410,6 +434,8 @@ def tile_fluxjointattention_pa_kernel(
             if k == 0:
                 qk_turn(1, 0)
                 qk_turn(1, 1)
+            if k in (5, 7):
+                spread_vbias((k - 5) // 2)
             if k < steps:
                 for i, prod in enumerate(prods):
                     v_mult(*prod, *((ps_v, "vacc") if i == 0 else (ps_acc, "acc")))
@@ -434,6 +460,8 @@ def tile_fluxjointattention_pa_kernel(
                 qk_rms((k - 2) // 2, k % 2)
             if k < steps:
                 qk_bias(k // 2, k % 2)
+            if k in (5, 7):
+                vbias_leave((k - 5) // 2)
             for s, c, j in rows:
                 if j == 0:
                     v_open(s, c)

@@ -81,16 +81,19 @@ def tile_fluxjointattention_pa_kernel(
                 out=brow[16 * s : 16 * s + 16, :],
                 in_=biases[s][0:2048].rearrange("(r f) -> r f", f=P),
             )
-        for m in range(4):
-            nc.scalar.dma_start(out=small[0:1, m * P : (m + 1) * P], in_=gains[m].unsqueeze(0))
-        for s in range(2):
-            nc.scalar.dma_start(
-                out=small[1 + 2 * s : 3 + 2 * s, :], in_=biases[s][2048:3072].rearrange("(r f) -> r f", f=512)
-            )
         ident = const.tile([P, P], F32, name="ident")
         make_identity(nc, ident[:])
         ident_b = const.tile([P, P], BF16, name="ident_b")
         nc.vector.tensor_copy(out=ident_b[:], in_=ident[:])
+
+        for m in range(4):
+            nc.gpsimd.dma_start(out=small[0:1, m * P : (m + 1) * P], in_=gains[m].unsqueeze(0))
+        for s in range(2):
+            nc.gpsimd.dma_start(
+                out=small[1 + 2 * s : 3 + 2 * s, :], in_=biases[s][2048:3072].rearrange("(r f) -> r f", f=512)
+            )
+        brow_f = const.tile([P, P], F32, name="brow_f")
+        nc.gpsimd.tensor_copy(out=brow_f[:], in_=brow[:])
 
         gain = const.tile([P, 4, P], BF16, name="gain")
         vbias = const.tile([P, 2, 1024], BF16, name="vbias")
@@ -176,8 +179,6 @@ def tile_fluxjointattention_pa_kernel(
         bias_t = const.tile([P, 32], F32, name="bias_t")
 
         def bias_columns():
-            brow_f = const.tile([P, P], F32, name="brow_f")
-            nc.scalar.copy(out=brow_f[:], in_=brow[:])
             bias_ps = ps_v.tile([P, 512], F32, name="bias_ps", tag="vacc")
             nc.tensor.transpose(bias_ps[:, 0:P], brow_f[:], ident[:])
             nc.scalar.copy(out=bias_t[:], in_=bias_ps[:, 0:32])
@@ -339,9 +340,9 @@ def tile_fluxjointattention_pa_kernel(
                 blk = 4 * bank + b
                 nc.vector.scalar_tensor_tensor(
                     out=mw[:, b, :, :],
-                    in0=y[:, b * P : (b + 1) * P].unsqueeze(1).to_broadcast([P, 2, P]),
+                    in0=tab[h // 8][:, blk, :, :],
                     scalar=rs[:, blk : blk + 1],
-                    in1=tab[h // 8][:, blk, :, :],
+                    in1=y[:, b * P : (b + 1) * P].unsqueeze(1).to_broadcast([P, 2, P]),
                     op0=ALU.mult,
                     op1=ALU.mult,
                 )
@@ -395,17 +396,15 @@ def tile_fluxjointattention_pa_kernel(
             qk_turn(0, s)
             qk_leave(0, s, s == 1)
         qk_quant(0)
-        bias_columns()
         x_pair(2)
         x_pair(3)
-        spread_gains()
         for s in range(2):
             load_w(s, 1, 0, 4)
         load_w(0, 5, 0, 4)
 
         units = [(0, 0), (0, 1), (1, 0), (1, 1)]
-        prep_steps = list(range(2, 28, 2)) + [27, 28, 29]
-        quant_steps = [10, 18, 26, 31]
+        prep_steps = list(range(2, 26, 2)) + [26, 27, 28, 28]
+        quant_steps = [10, 18, 26, 30]
         block_steps = list(range(11, 31, 2)) + [28, 30, 31, 32, 32, 33]
         v_rows = [(s, c, j) for s, c in units for j in range(4)]
         v_prods = [(s, c, t) for s, c in units for t in range(TOKEN_BLOCKS[s])]
@@ -426,14 +425,14 @@ def tile_fluxjointattention_pa_kernel(
                     v_store(prod[0], prod[1])
             if k in quant_steps:
                 v_quant(*units[quant_steps.index(k)])
-            if k < 2:
-                for c in range(2):
-                    table(nc.vector, 0, k, c)
             if k < steps:
                 qk_mult(k // 2, k % 2)
             if k == 0:
+                bias_columns()
                 qk_turn(1, 0)
+                spread_gains()
                 qk_turn(1, 1)
+                qk_bias(0, 0)
             if k in (5, 7):
                 spread_vbias((k - 5) // 2)
             if k < steps:
@@ -448,6 +447,9 @@ def tile_fluxjointattention_pa_kernel(
                 if k == 1:
                     qk_turn(2, 0)
                 qk_turn(*ahead)
+            if k < 2:
+                for c in range(2):
+                    table(nc.vector, 0, k, c)
             if k == 0:
                 qk_leave(1, 0)
             if k >= 2:
@@ -458,7 +460,7 @@ def tile_fluxjointattention_pa_kernel(
                 qk_leave(*ahead_before)
             if k >= 2:
                 qk_rms((k - 2) // 2, k % 2)
-            if k < steps:
+            if 0 < k < steps:
                 qk_bias(k // 2, k % 2)
             if k in (5, 7):
                 vbias_leave((k - 5) // 2)

@@ -74,45 +74,47 @@ def tile_fluxjointattention_pa_kernel(
         nc.scalar.activation(out=warm[:], in_=eps_t[:], func=ACT.Abs_reciprocal_sqrt)
         brow = const.tile([P, P], BF16, name="brow")
         nc.vector.memset(brow[:], 0.0)
-        small = const.tile([P, 512], BF16, name="small")
-        nc.vector.memset(small[:], 0.0)
+        rows_g = const.tile([P, 512], BF16, name="rows_g")
+        nc.vector.memset(rows_g[:], 0.0)
+        rows_v = const.tile([P, 512], BF16, name="rows_v")
+        nc.vector.memset(rows_v[:], 0.0)
+        ident = const.tile([P, P], F32, name="ident")
+        make_identity(nc, ident[:])
+        ident_b = const.tile([P, P], BF16, name="ident_b")
+        nc.vector.tensor_copy(out=ident_b[:], in_=ident[:])
         for s in range(2):
             nc.scalar.dma_start(
                 out=brow[16 * s : 16 * s + 16, :],
                 in_=biases[s][0:2048].rearrange("(r f) -> r f", f=P),
             )
-        ident = const.tile([P, P], F32, name="ident")
-        make_identity(nc, ident[:])
-        ident_b = const.tile([P, P], BF16, name="ident_b")
-        nc.vector.tensor_copy(out=ident_b[:], in_=ident[:])
-
         for m in range(4):
-            nc.gpsimd.dma_start(out=small[0:1, m * P : (m + 1) * P], in_=gains[m].unsqueeze(0))
-        for s in range(2):
-            nc.gpsimd.dma_start(
-                out=small[1 + 2 * s : 3 + 2 * s, :], in_=biases[s][2048:3072].rearrange("(r f) -> r f", f=512)
-            )
+            queue = (nc.scalar, nc.gpsimd)[m % 2]
+            queue.dma_start(out=rows_g[0:1, m * P : (m + 1) * P], in_=gains[m].unsqueeze(0))
         brow_f = const.tile([P, P], F32, name="brow_f")
         nc.gpsimd.tensor_copy(out=brow_f[:], in_=brow[:])
+        for s in range(2):
+            nc.gpsimd.dma_start(
+                out=rows_v[2 * s : 2 * s + 2, :], in_=biases[s][2048:3072].rearrange("(r f) -> r f", f=512)
+            )
 
         gain = const.tile([P, 4, P], BF16, name="gain")
         vbias = const.tile([P, 2, 1024], BF16, name="vbias")
         rope = const.tile([P, 8, 256], BF16, name="rope")
 
-        def spread(bank, row):
+        def spread(bank, rows, row):
             nc.tensor.matmul(
-                out=bank, lhsT=ident_b[:, row : row + 1].to_broadcast([P, P]), rhs=small[:], start=True, stop=True
+                out=bank, lhsT=ident_b[:, row : row + 1].to_broadcast([P, P]), rhs=rows[:], start=True, stop=True
             )
 
         def spread_gains():
             bank = ps_v.tile([P, 512], BF16, name="bank_gain", tag="vacc")
-            spread(bank[:], 0)
+            spread(bank[:], rows_g, 0)
             nc.vector.tensor_copy(out=gain[:].rearrange("p m f -> p (m f)"), in_=bank[:])
 
         def spread_vbias(s):
             bank = ps_v.tile([P, 1024], BF16, name="bank_vbias", tag="vacc")
             for c in range(2):
-                spread(bank[:, c * 512 : (c + 1) * 512], 1 + 2 * s + c)
+                spread(bank[:, c * 512 : (c + 1) * 512], rows_v, 2 * s + c)
             st[("vbias", s)] = bank
 
         def vbias_leave(s):
@@ -235,8 +237,8 @@ def tile_fluxjointattention_pa_kernel(
         def v_add(s, c, t):
             nc.vector.tensor_tensor(
                 out=vst[("out", s, c)][:, :, t, :],
-                in0=vst[("acc", s, c, t)][:].rearrange("p (h f) -> p h f", h=4),
-                in1=vbias[:, s, c * 512 : (c + 1) * 512].rearrange("p (h f) -> p h f", h=4),
+                in0=vbias[:, s, c * 512 : (c + 1) * 512].rearrange("p (h f) -> p h f", h=4),
+                in1=vst[("acc", s, c, t)][:].rearrange("p (h f) -> p h f", h=4),
                 op=ALU.add,
             )
 
@@ -435,12 +437,12 @@ def tile_fluxjointattention_pa_kernel(
                 qk_bias(0, 0)
             if k in (5, 7):
                 spread_vbias((k - 5) // 2)
-            if k < steps:
+            if k < steps - 2:
                 for i, prod in enumerate(prods):
                     v_mult(*prod, *((ps_v, "vacc") if i == 0 else (ps_acc, "acc")))
             if 0 < k <= steps:
                 qk_back((k - 1) // 2, (k - 1) % 2)
-            if k >= steps:
+            if k >= steps - 2:
                 for i, prod in enumerate(prods):
                     v_mult(*prod, *((ps_v, "vacc") if i == 0 else (ps_acc, "acc")))
             if 0 < k and ahead[0] < HEADS:

@@ -298,13 +298,14 @@ def tile_fluxjointattention_pa_kernel(
             st[("yt", h, bank)] = yt
 
         def qk_back(h, bank):
+            heater = int(bank == 1 or h < 5)
             yt = st[("yt", h, bank)]
             y = ps_y.tile([P, 512], F32, name="y", tag="y")
-            for b in range(1):
+            for b in range(heater):
                 nc.tensor.matmul(
                     out=y[:, b * P : (b + 1) * P], lhsT=yt[:, b * P : (b + 1) * P], rhs=ident[:], start=True, stop=True
                 )
-            for b in range(1, 4):
+            for b in range(heater, 4):
                 nc.tensor.transpose(y[:, b * P : (b + 1) * P], yt[:, b * P : (b + 1) * P], ident[:])
             st[("y", h, bank)] = y
 
@@ -361,6 +362,18 @@ def tile_fluxjointattention_pa_kernel(
                 in1=mw[:, :, 1, :].rearrange("p b (j c) -> p b j c", c=2)[:, :, :, ::-1],
                 op=ALU.add,
             )
+
+        def qk_store_last(bank):
+            o = st[("o", HEADS - 1)]
+            t0, t1 = ((0, 4), (4, 6))[bank]
+            nc.sync.dma_start(
+                out=out_1[0, 7, 256:1024, :].rearrange("(p t) f -> p t f", t=6)[:, t0:t1, :], in_=o[:, t0:t1, :]
+            )
+            if bank == 1:
+                nc.sync.dma_start(
+                    out=out_1[0, 7, 0:256, :].rearrange("(p t) f -> p (t f)", t=2),
+                    in_=o[:, 6:8, :].rearrange("p t f -> p (t f)"),
+                )
 
         def qk_store(h):
             dst = qk_out[h // 8]
@@ -477,13 +490,16 @@ def tile_fluxjointattention_pa_kernel(
                 if k in (4, 6, 8, 10):
                     table(nc.gpsimd, 1, (k - 4) // 4, (k // 2) % 2)
                 qk_add((k - 2) // 2, k % 2)
-                if k % 2 == 1:
+                if k >= steps:
+                    qk_store_last(k % 2)
+                elif k % 2 == 1:
                     qk_store((k - 2) // 2)
             if k in (4, 12):
                 for s in range(2):
                     load_w(s, 2 + k // 12, 0, 4)
-            if k in (7, 15):
-                load_w(1, 4 + k // 15, 0, 4)
+            for c in range(2):
+                if k == prep_steps[4 * c + 3]:
+                    load_w(1, 4 + c, 0, 4)
         for i in range(16):
             if block_steps[i] == steps + 1:
                 v_add(*v_prods[i])

@@ -298,7 +298,7 @@ def tile_fluxjointattention_pa_kernel(
             st[("yt", h, bank)] = yt
 
         def qk_back(h, bank):
-            heater = int(bank == 1 or h < 5)
+            heater = int(h < 5)
             yt = st[("yt", h, bank)]
             y = ps_y.tile([P, 512], F32, name="y", tag="y")
             for b in range(heater):
@@ -451,13 +451,13 @@ def tile_fluxjointattention_pa_kernel(
             if k in (5, 7):
                 spread_vbias((k - 5) // 2)
             if k < steps - 2:
-                for i, prod in enumerate(prods):
-                    v_mult(*prod, *((ps_v, "vacc") if i == 0 else (ps_acc, "acc")))
+                for prod in prods:
+                    v_mult(*prod, *((ps_prep, "prep") if k >= 30 else (ps_v, "vacc")))
             if 0 < k <= steps:
                 qk_back((k - 1) // 2, (k - 1) % 2)
             if k >= steps - 2:
-                for i, prod in enumerate(prods):
-                    v_mult(*prod, *((ps_v, "vacc") if i == 0 else (ps_acc, "acc")))
+                for prod in prods:
+                    v_mult(*prod, *((ps_prep, "prep") if k >= 30 else (ps_v, "vacc")))
             if 0 < k and ahead[0] < HEADS:
                 if k == 1:
                     qk_turn(2, 0)

from contextlib import ExitStack

import concourse.mybir as mybir
from concourse.masks import make_identity

FLOPS = 2 * 1024 * 1024 * 3072

F32 = mybir.dt.float32
BF16 = mybir.dt.bfloat16
U32 = mybir.dt.uint32
U8 = mybir.dt.uint8
FP8X4 = mybir.dt.float8_e4m3fn_x4
ACT = mybir.ActivationFunctionType
ALU = mybir.AluOpType

P = 128
K = 1024
HEADS = 16
EPS = 1e-6
TOKEN_BLOCKS = (6, 2)
FIRST_BLOCK = (0, 6)
BIAS_PARTS = (((0, 512, 0),), ((0, 256, 0), (256, 256, 1)))


def x_word(blk, g):
    return (blk // 2) * 512 + g * 256 + (blk % 2) * P


def tile_fluxjointattention_pa_kernel(
    tc,
    hidden_states_a,
    hidden_states_b,
    image_rotary_emb,
    a_qkv_w,
    a_qkv_b,
    b_qkv_w,
    b_qkv_b,
    norm_q_a_w,
    norm_k_a_w,
    norm_q_b_w,
    norm_k_b_w,
    out_0,
    out_1,
    out_2,
):
    nc = tc.nc
    with ExitStack() as ctx:
        ctx.enter_context(tc.manual_schedule())
        const = ctx.enter_context(tc.tile_pool(name="const", bufs=1))
        raws = ctx.enter_context(tc.tile_pool(name="raws", bufs=4))
        grps = ctx.enter_context(tc.tile_pool(name="grps", bufs=3))
        cods = ctx.enter_context(tc.tile_pool(name="cods", bufs=4))
        work = ctx.enter_context(tc.tile_pool(name="work", bufs=4))
        outs = ctx.enter_context(tc.tile_pool(name="outs", bufs=2))
        ps_prep = ctx.enter_context(tc.psum_pool(name="psprep", bufs=2))
        ps_acc = ctx.enter_context(tc.psum_pool(name="psacc", bufs=2))
        ps_v = ctx.enter_context(tc.psum_pool(name="psv", bufs=1))
        ps_y = ctx.enter_context(tc.psum_pool(name="psy", bufs=3))

        xa_v = hidden_states_a.rearrange("o (p t) k -> p (o t) k", t=6)
        xb_v = hidden_states_b.rearrange("o (p t) k -> p (o t) k", t=2)
        w_v = [
            a_qkv_w.rearrange("(n p) k -> p n k", p=P),
            b_qkv_w.rearrange("(n p) k -> p n k", p=P),
        ]
        rope_v = image_rotary_emb.rearrange("a b s j i c -> (a b s) (j i c)")
        biases = [a_qkv_b, b_qkv_b]
        gains = [norm_q_a_w, norm_k_a_w, norm_q_b_w, norm_k_b_w]
        qk_out = [out_0, out_1]

        eps_t = const.tile([P, 1], F32, name="eps_t")
        nc.vector.memset(eps_t[:], EPS)
        warm = const.tile([P, 1], F32, name="warm")
        nc.scalar.activation(out=warm[:], in_=eps_t[:], func=ACT.Abs_reciprocal_sqrt)
        brow = const.tile([P, P], BF16, name="brow")
        nc.vector.memset(brow[:], 0.0)
        rows_g = const.tile([P, 512], BF16, name="rows_g")
        nc.vector.memset(rows_g[:], 0.0)
        rows_v = const.tile([P, 512], BF16, name="rows_v")
        nc.vector.memset(rows_v[:], 0.0)
        ident = const.tile([P, P], F32, name="ident")
        make_identity(nc, ident[:])
        ident_b = const.tile([P, P], BF16, name="ident_b")
        nc.vector.tensor_copy(out=ident_b[:], in_=ident[:])
        for s in range(2):
            nc.scalar.dma_start(
                out=brow[16 * s : 16 * s + 16, :],
                in_=biases[s][0:2048].rearrange("(r f) -> r f", f=P),
            )
        for m in range(4):
            queue = (nc.scalar, nc.gpsimd)[m % 2]
            queue.dma_start(out=rows_g[0:1, m * P : (m + 1) * P], in_=gains[m].unsqueeze(0))
        brow_f = const.tile([P, P], F32, name="brow_f")
        nc.gpsimd.tensor_copy(out=brow_f[:], in_=brow[:])
        for s in range(2):
            nc.gpsimd.dma_start(
                out=rows_v[2 * s : 2 * s + 2, :], in_=biases[s][2048:3072].rearrange("(r f) -> r f", f=512)
            )

        gain = const.tile([P, 4, P], BF16, name="gain")
        vbias = const.tile([P, 2, 1024], BF16, name="vbias")
        rope = const.tile([P, 8, 256], BF16, name="rope")

        def spread(bank, rows, row):
            nc.tensor.matmul(
                out=bank, lhsT=ident_b[:, row : row + 1].to_broadcast([P, P]), rhs=rows[:], start=True, stop=True
            )

        def spread_gains():
            bank = ps_v.tile([P, 512], BF16, name="bank_gain", tag="vacc")
            spread(bank[:], rows_g, 0)
            nc.vector.tensor_copy(out=gain[:].rearrange("p m f -> p (m f)"), in_=bank[:])

        def spread_vbias(s):
            bank = ps_v.tile([P, 1024], BF16, name="bank_vbias", tag="vacc")
            for c in range(2):
                spread(bank[:, c * 512 : (c + 1) * 512], rows_v, 2 * s + c)
            st[("vbias", s)] = bank

        def vbias_leave(s):
            nc.scalar.copy(out=vbias[:, s, :], in_=st[("vbias", s)][:])

        st = {}

        def load_rope():
            nc.sync.dma_start(out=rope[:, 0:6, :], in_=rope_v[256:1024, :].rearrange("(p t) e -> p t e", t=6))
            nc.sync.dma_start(out=rope[:, 6:8, :], in_=rope_v[0:256, :].rearrange("(p t) e -> p t e", t=2))

        def turn(pool, tag, rows):
            bank = pool.tile([P, 512], F32, name="bank_" + tag, tag=tag)
            words = rows.bitcast(F32)
            for gu in range(4):
                g, u = divmod(gu, 2)
                nc.tensor.transpose(
                    bank[:, gu * P : (gu + 1) * P], words[:, 256 * g + u : 256 * (g + 1) : 2], ident[:]
                )
            return bank

        def leave(bank, dst, vector=False):
            words = bank[:].rearrange("p (g u n) -> p g n u", g=2, u=2)
            if vector:
                nc.vector.tensor_copy(out=dst, in_=words)
            else:
                nc.scalar.copy(out=dst, in_=words)

        def quant(codes, scales, grp, w0, w1, g0):
            nc.vector.quantize_mx(
                out=codes[:, w0:w1].bitcast(FP8X4),
                scales=scales[:, w0:w1],
                in_=grp[:, g0 : g0 + 4 * (w1 - w0)],
            )

        raw_w = {}

        def load_w(s, chunk, j0, j1):
            if j0 == 0:
                if chunk < 4:
                    raw_w[(s, chunk)] = raws.tile([P, 4, K], BF16, name="raw_w%d_%d" % (s, chunk), tag="raw")
                else:
                    raw_w[(s, chunk)] = raws.tile([P, 4, K], BF16, name="raw_w%d_%d" % (s, chunk), tag="rawv", bufs=2)
            nc.sync.dma_start(out=raw_w[(s, chunk)][:, j0:j1, :], in_=w_v[s][:, 4 * chunk + j0 : 4 * chunk + j1, :])

        raw_x = [raws.tile([P, 4, K], BF16, name="raw_x%d" % i, tag="raw") for i in range(2)]
        x_codes = const.tile([P, 2048], U32, name="x_codes", align_bytes=64)
        x_scale = const.tile([P, 2048], U8, name="x_scale", align_bytes=64)
        xg = [grps.tile([P, 4096], BF16, name="xg%d" % i, tag="grp8", align_bytes=64) for i in range(2)]

        def load_x(pair):
            src = (xa_v[:, 0:2, :], xa_v[:, 2:4, :], xa_v[:, 4:6, :], xb_v)[pair]
            nc.sync.dma_start(out=raw_x[pair // 2][:, 2 * (pair % 2) : 2 * (pair % 2) + 2, :], in_=src)

        def x_prep(blk, vector):
            pool, tag = ((ps_y, "y"), (ps_prep, "prep"), (ps_acc, "acc"), (ps_y, "y"))[blk // 2]
            bank = turn(pool, tag, raw_x[blk // 4][:, blk % 4, :])
            pairs = xg[blk // 4][:].bitcast(F32).rearrange("p (c g n u) -> p c g n u", c=2, g=2, u=2)
            leave(bank, pairs[:, (blk // 2) % 2, :, (blk % 2) * P : (blk % 2 + 1) * P, :], vector)

        def x_quant(pair):
            quant(x_codes, x_scale, xg[pair // 2], 512 * pair, 512 * pair + 512, 2048 * (pair % 2))

        bias_t = const.tile([P, 32], F32, name="bias_t")

        def bias_columns():
            bias_ps = ps_v.tile([P, 512], F32, name="bias_ps", tag="vacc")
            nc.tensor.transpose(bias_ps[:, 0:P], brow_f[:], ident[:])
            nc.scalar.copy(out=bias_t[:], in_=bias_ps[:, 0:32])

        gain_p = gain[:].rearrange("p m (j c) -> p m j c", c=2)
        tab = [const.tile([P, 8, 2, P], F32, name="tab%d" % kind) for kind in range(2)]
        rope_q = rope[:].rearrange("p t (j q) -> p t j q", q=4)

        def table(engine, kind, s, c):
            b0 = FIRST_BLOCK[s]
            b1 = b0 + TOKEN_BLOCKS[s]
            engine.tensor_tensor(
                out=tab[kind][:, b0:b1, c, :].rearrange("p t (j c) -> p t j c", c=2),
                in0=rope_q[:, b0:b1, :, (slice(0, 4, 3), slice(2, 0, -1))[c]],
                in1=gain_p[:, 2 * s + kind, :, :].unsqueeze(1).to_broadcast([P, b1 - b0, 64, 2]),
                op=ALU.mult,
            )

        vst = {}

        def v_open(s, c):
            vst[("grp", s, c)] = grps.tile([P, 4096], BF16, name="vg", tag="grp8", align_bytes=64)

        def v_turn(s, c, j, pool, tag):
            vst[("bank", s, c, j)] = turn(pool, tag, raw_w[(s, 4 + c)][:, j, :])

        def v_leave(s, c, j):
            vg_v = vst[("grp", s, c)][:].bitcast(F32).rearrange("p (g n u) -> p g n u", g=2, u=2)
            leave(vst[("bank", s, c, j)], vg_v[:, :, j * P : (j + 1) * P, :])

        def v_quant(s, c):
            vc = const.tile([P, 1024], U32, name="vc%d%d" % (s, c), align_bytes=64)
            vs = const.tile([P, 1024], U8, name="vs%d%d" % (s, c), align_bytes=64)
            quant(vc, vs, vst[("grp", s, c)], 0, 1024, 0)
            vst[("codes", s, c)] = (vc, vs)
            vst[("out", s, c)] = outs.tile([P, 4, TOKEN_BLOCKS[s], P], F32, name="ov%d" % s)

        def v_mult(s, c, t, pool, tag):
            vc, vs = vst[("codes", s, c)]
            acc = pool.tile([P, 512], F32, name="vacc", tag=tag)
            for g in range(2):
                xo = x_word(FIRST_BLOCK[s] + t, g)
                nc.tensor.matmul_mx(
                    out=acc[:],
                    lhsT=x_codes[:, xo : xo + P].bitcast(FP8X4),
                    lhsT_scale=x_scale[:, xo : xo + P],
                    rhs=vc[:, g * 512 : (g + 1) * 512].bitcast(FP8X4),
                    rhs_scale=vs[:, g * 512 : (g + 1) * 512],
                    start=(g == 0),
                    stop=(g == 1),
                )
            vst[("acc", s, c, t)] = acc

        def v_add(s, c, t):
            nc.vector.tensor_tensor(
                out=vst[("out", s, c)][:, :, t, :],
                in0=vbias[:, s, c * 512 : (c + 1) * 512].rearrange("p (h f) -> p h f", h=4),
                in1=vst[("acc", s, c, t)][:].rearrange("p (h f) -> p h f", h=4),
                op=ALU.add,
            )

        def v_store(s, c):
            lo, hi = ((256, 1024), (0, 256))[s]
            nc.sync.dma_start(
                out=out_2[0, 4 * c : 4 * c + 4, lo:hi, :].rearrange("h (p t) f -> p h (t f)", t=TOKEN_BLOCKS[s]),
                in_=vst[("out", s, c)][:].rearrange("p h t f -> p h (t f)"),
            )

        def qk_turn(h, s):
            st[("bank", h, s)] = turn(ps_prep, "prep", raw_w[(s, h // 4)][:, h % 4, :])

        def qk_leave(h, s, vector=False):
            if s == 0:
                st[("grp", h)] = grps.tile([P, 2048], BF16, name="grp", tag="grp4", align_bytes=64, bufs=3)
            grp_v = st[("grp", h)][:].bitcast(F32).rearrange("p (s g n u) -> p s g n u", s=2, g=2, u=2)
            leave(st[("bank", h, s)], grp_v[:, s, :, :, :], vector)

        def qk_quant(h, s0=0, s1=2):
            if s0 == 0:
                wc = cods.tile([P, 512], U32, name="wc", align_bytes=64)
                ws = cods.tile([P, 512], U8, name="ws", align_bytes=64)
                st[("codes", h)] = (wc, ws)
            quant(*st[("codes", h)], st[("grp", h)], 256 * s0, 256 * s1, 1024 * s0)

        def qk_mult(h, bank):
            wc, ws = st[("codes", h)]
            acc = ps_acc.tile([P, 512], F32, name="acc", tag="acc")
            for half in range(2):
                s = int(2 * bank + half == 3)
                for g in range(2):
                    wo = (2 * s + g) * P
                    xo = x_word(4 * bank + 2 * half, g)
                    nc.tensor.matmul_mx(
                        out=acc[:, half * 256 : (half + 1) * 256],
                        lhsT=wc[:, wo : wo + P].bitcast(FP8X4),
                        lhsT_scale=ws[:, wo : wo + P],
                        rhs=x_codes[:, xo : xo + 256].bitcast(FP8X4),
                        rhs_scale=x_scale[:, xo : xo + 256],
                        start=(g == 0),
                        stop=(g == 1),
                    )
            st[("acc", h, bank)] = acc

        def qk_bias(h, bank):
            acc = st[("acc", h, bank)]
            yt = work.tile([P, 512], F32, name="yt")
            for c0, n, s in BIAS_PARTS[bank]:
                nc.scalar.activation(
                    out=yt[:, c0 : c0 + n],
                    in_=acc[:, c0 : c0 + n],
                    func=ACT.Identity,
                    bias=bias_t[:, 16 * s + h : 16 * s + h + 1],
                    scale=1.0,
                )
            st[("yt", h, bank)] = yt

        def qk_back(h, bank):
            heater = int(h < 5)
            yt = st[("yt", h, bank)]
            y = ps_y.tile([P, 512], F32, name="y", tag="y")
            for b in range(heater):
                nc.tensor.matmul(
                    out=y[:, b * P : (b + 1) * P], lhsT=yt[:, b * P : (b + 1) * P], rhs=ident[:], start=True, stop=True
                )
            for b in range(heater, 4):
                nc.tensor.transpose(y[:, b * P : (b + 1) * P], yt[:, b * P : (b + 1) * P], ident[:])
            st[("y", h, bank)] = y

        unused = const.tile([P, 8, P], BF16, name="unused")

        def qk_square(h, bank):
            if bank == 0:
                st[("ss", h)] = work.tile([P, 8], F32, name="ss")
            y = st[("y", h, bank)]
            for b in range(4):
                blk = 4 * bank + b
                nc.scalar.activation(
                    out=unused[:, blk, :],
                    in_=y[:, b * P : (b + 1) * P],
                    func=ACT.Square,
                    accum_out=st[("ss", h)][:, blk : blk + 1],
                )

        def qk_rms(h, bank):
            if bank == 0:
                st[("rs", h)] = work.tile([P, 8], F32, name="rs")
            nc.scalar.activation(
                out=st[("rs", h)][:, 4 * bank : 4 * bank + 4],
                in_=st[("ss", h)][:, 4 * bank : 4 * bank + 4],
                func=ACT.Abs_reciprocal_sqrt,
                bias=eps_t[:],
                scale=1.0 / P,
            )

        def qk_rope(h, bank):
            y = st[("y", h, bank)]
            rs = st[("rs", h)]
            mw = work.tile([P, 4, 2, P], F32, name="mw")
            for b in range(4):
                blk = 4 * bank + b
                nc.vector.scalar_tensor_tensor(
                    out=mw[:, b, :, :],
                    in0=tab[h // 8][:, blk, :, :],
                    scalar=rs[:, blk : blk + 1],
                    in1=y[:, b * P : (b + 1) * P].unsqueeze(1).to_broadcast([P, 2, P]),
                    op0=ALU.mult,
                    op1=ALU.mult,
                )
            st[("m", h, bank)] = mw

        def qk_add(h, bank):
            if bank == 0:
                st[("o", h)] = outs.tile([P, 8, P], F32, name="o", bufs=3)
            mw = st[("m", h, bank)]
            engine = nc.vector if (h, bank) == (HEADS - 1, 1) else nc.gpsimd
            engine.tensor_tensor(
                out=st[("o", h)][:, 4 * bank : 4 * bank + 4, :].rearrange("p b (j c) -> p b j c", c=2),
                in0=mw[:, :, 0, :].rearrange("p b (j c) -> p b j c", c=2),
                in1=mw[:, :, 1, :].rearrange("p b (j c) -> p b j c", c=2)[:, :, :, ::-1],
                op=ALU.add,
            )

        def qk_store_last(bank):
            o = st[("o", HEADS - 1)]
            t0, t1 = ((0, 4), (4, 6))[bank]
            nc.sync.dma_start(
                out=out_1[0, 7, 256:1024, :].rearrange("(p t) f -> p t f", t=6)[:, t0:t1, :], in_=o[:, t0:t1, :]
            )
            if bank == 1:
                nc.sync.dma_start(
                    out=out_1[0, 7, 0:256, :].rearrange("(p t) f -> p (t f)", t=2),
                    in_=o[:, 6:8, :].rearrange("p t f -> p (t f)"),
                )

        def qk_store(h):
            dst = qk_out[h // 8]
            o = st[("o", h)]
            nc.sync.dma_start(
                out=dst[0, h % 8, 256:1024, :].rearrange("(p t) f -> p (t f)", t=6),
                in_=o[:, 0:6, :].rearrange("p t f -> p (t f)"),
            )
            nc.sync.dma_start(
                out=dst[0, h % 8, 0:256, :].rearrange("(p t) f -> p (t f)", t=2),
                in_=o[:, 6:8, :].rearrange("p t f -> p (t f)"),
            )

        load_x(0)
        load_x(1)
        for s in range(2):
            load_w(s, 0, 0, 1)
        load_x(2)
        load_x(3)
        for s in range(2):
            load_w(s, 0, 1, 2)
        load_rope()
        for s in range(2):
            load_w(s, 0, 2, 4)
        load_w(0, 4, 0, 4)

        def x_pair(pair):
            for blk in (2 * pair, 2 * pair + 1):
                x_prep(blk, blk % 2 == 1 and pair < 3)
            x_quant(pair)

        x_pair(0)
        x_pair(1)
        for s in range(2):
            qk_turn(0, s)
            qk_leave(0, s, s == 1)
        qk_quant(0)
        x_pair(2)
        x_pair(3)
        for s in range(2):
            load_w(s, 1, 0, 4)
        load_w(0, 5, 0, 4)

        units = [(0, 0), (0, 1), (1, 0), (1, 1)]
        prep_steps = list(range(2, 26, 2)) + [26, 27, 28, 28]
        quant_steps = [10, 18, 26, 30]
        block_steps = list(range(11, 31, 2)) + [28, 30, 31, 32, 32, 33]
        v_rows = [(s, c, j) for s, c in units for j in range(4)]
        v_prods = [(s, c, t) for s, c in units for t in range(TOKEN_BLOCKS[s])]

        steps = 2 * HEADS
        for k in range(steps + 2):
            rows = [v_rows[i] for i in range(16) if prep_steps[i] == k]
            rows_before = [v_rows[i] for i in range(16) if prep_steps[i] == k - 1]
            prods = [v_prods[i] for i in range(16) if block_steps[i] == k]
            prods_before = [v_prods[i] for i in range(16) if block_steps[i] == k - 1]
            ahead = divmod(k + 4, 2)
            ahead_before = divmod(k + 3, 2)
            if k % 2 == 1 and k + 1 < steps:
                qk_quant((k + 1) // 2)
            for prod in prods_before:
                v_add(*prod)
                if prod[2] == TOKEN_BLOCKS[prod[0]] - 1:
                    v_store(prod[0], prod[1])
            if k in quant_steps:
                v_quant(*units[quant_steps.index(k)])
            if k < steps:
                qk_mult(k // 2, k % 2)
            if k == 0:
                bias_columns()
                qk_turn(1, 0)
                spread_gains()
                qk_turn(1, 1)
                qk_bias(0, 0)
            if k in (5, 7):
                spread_vbias((k - 5) // 2)
            if k < steps - 2:
                for prod in prods:
                    v_mult(*prod, *((ps_prep, "prep") if k >= 30 else (ps_v, "vacc")))
            if 0 < k <= steps:
                qk_back((k - 1) // 2, (k - 1) % 2)
            if k >= steps - 2:
                for prod in prods:
                    v_mult(*prod, *((ps_prep, "prep") if k >= 30 else (ps_v, "vacc")))
            if 0 < k and ahead[0] < HEADS:
                if k == 1:
                    qk_turn(2, 0)
                qk_turn(*ahead)
            if k < 2:
                for c in range(2):
                    table(nc.vector, 0, k, c)
            if k == 0:
                qk_leave(1, 0)
            if k >= 2:
                qk_square((k - 2) // 2, k % 2)
            if k != 1 and ahead_before[0] < HEADS:
                if k == 2:
                    qk_leave(2, 0)
                qk_leave(*ahead_before)
            if k >= 2:
                qk_rms((k - 2) // 2, k % 2)
            if 0 < k < steps:
                qk_bias(k // 2, k % 2)
            if k in (5, 7):
                vbias_leave((k - 5) // 2)
            for s, c, j in rows:
                if j == 0:
                    v_open(s, c)
                v_turn(s, c, j, ps_prep, "prep")
            for s, c, j in rows_before:
                v_leave(s, c, j)
            if k >= 2:
                qk_rope((k - 2) // 2, k % 2)
                if k in (4, 6, 8, 10):
                    table(nc.gpsimd, 1, (k - 4) // 4, (k // 2) % 2)
                qk_add((k - 2) // 2, k % 2)
                if k >= steps:
                    qk_store_last(k % 2)
                elif k % 2 == 1:
                    qk_store((k - 2) // 2)
            if k in (4, 12):
                for s in range(2):
                    load_w(s, 2 + k // 12, 0, 4)
            for c in range(2):
                if k == prep_steps[4 * c + 3]:
                    load_w(1, 4 + c, 0, 4)
        for i in range(16):
            if block_steps[i] == steps + 1:
                v_add(*v_prods[i])
        v_store(1, 1)
